import numpy as np
import ml_dtypes


def mxq(x, axis, fmt="e4m3"):
    dtype, down = {"e4m3": (ml_dtypes.float8_e4m3fn, 7), "e5m2": (ml_dtypes.float8_e5m2, 14)}[fmt]
    v = np.moveaxis(np.asarray(x, np.float32).astype(ml_dtypes.bfloat16).astype(np.float64), axis, -1)
    blocks = v.reshape(v.shape[:-1] + (-1, 32))
    amax = np.abs(blocks).max(-1, keepdims=True)
    byte = np.maximum(np.where(amax > 0, np.frexp(amax)[1] - 1 + 127, 0) - down, 1)
    scale = np.exp2(byte - 127.0)
    codes = (blocks / scale).astype(np.float32).astype(dtype).astype(np.float64)
    return np.moveaxis((codes * scale).reshape(v.shape), -1, axis)


WIDE = False


def mx_kscale(k):
    if not WIDE:
        return np.ones(k)
    levels = np.array([10, -10, 5, -5, 0])
    a = np.random.permutation(np.resize(levels, k // 512 * 4)).reshape(k // 512, 4)
    idx = np.arange(k)
    return np.exp2(a[idx // 512, idx % 128 // 32])


BF16 = ml_dtypes.bfloat16


def bf(x):
    return np.asarray(x, np.float32).astype(BF16)


def f64(x):
    return np.asarray(x).astype(np.float64)


B, L, C, H, DH, AX = 2, 128, 8192, 16, 96, 3
D3 = DH // AX
HALF = D3 // 2
ROPE_BASE = 10000.0
COORD_MAX = 10.0


def rope_3d(x, coords):
    inv_freq = 1.0 / (ROPE_BASE ** (np.arange(HALF) / HALF))
    ang = coords[..., None] * inv_freq
    cos = np.cos(ang)[:, None]
    sin = np.sin(ang)[:, None]
    xr = x.reshape(B, H, L, AX, D3)
    x1, x2 = xr[..., :HALF], xr[..., HALF:]
    out = np.concatenate([x1 * cos - x2 * sin, x1 * sin + x2 * cos], axis=-1)
    return out.reshape(B, H, L, DH)


def setup_inputs():
    s = mx_kscale(C)
    return {"x_in": bf(np.random.standard_normal((B, L, C)) * s),
            "coords": bf(np.random.uniform(size=(B, L, AX)) * COORD_MAX),
            "w": bf(np.random.standard_normal((H * DH, C)) * 1.5 / np.sqrt(C) / s)}


def reference(x_in, coords, w):
    p = mxq(f64(x_in), 2, "e4m3") @ mxq(f64(w), 1, "e4m3").T
    p = p.reshape(B, L, H, DH).transpose(0, 2, 1, 3)
    return rope_3d(p, f64(coords))

@@ -1,0 +1,278 @@
+from contextlib import ExitStack
+import math
+
+import concourse.mybir as mybir
+from concourse.masks import make_identity
+
+F32 = mybir.dt.float32
+BF16 = mybir.dt.bfloat16
+U32 = mybir.dt.uint32
+U8 = mybir.dt.uint8
+FP8X4 = mybir.dt.float8_e4m3fn_x4
+ALU = mybir.AluOpType
+ACT = mybir.ActivationFunctionType
+
+P = 128
+BATCHES, TOKENS, K = 2, 128, 8192
+HEADS, HEAD_DIM, AXES, PAIRS = 16, 96, 3, 16
+FEATURES = HEADS * HEAD_DIM
+ROPE_BASE = 10000.0
+
+K_PASS = 512
+ROWS = 256
+ROW_TILES = ROWS // P
+PASSES_RUN = 8
+K_RUN = PASSES_RUN * K_PASS
+HALVES = K // K_RUN
+GROUPS = FEATURES // ROWS
+BANK = 512
+PAIR_WORDS = 2 * ROWS
+
+RAW_BUFS = 6
+TRANSPOSE_BANKS = 6
+VECTOR_PASS = 3
+
+FLOPS = 2 * BATCHES * TOKENS * FEATURES * K
+
+ROUND_MAGIC = 1.5 * 2.0**23
+
+
+def leading_bits(value, bits):
+    scale = 1.0
+    while abs(value) * scale < 2.0 ** (bits - 1):
+        scale *= 2.0
+    while abs(value) * scale >= 2.0**bits:
+        scale /= 2.0
+    return round(value * scale) / scale
+
+
+def build_rotation_tables(nc, consts, coords_bf):
+    columns = BATCHES * AXES
+    shape = [P, columns, PAIRS]
+
+    freq_head = consts.tile([P, PAIRS], F32)
+    freq_tail = consts.tile([P, PAIRS], F32)
+    for i in range(PAIRS):
+        inv_freq = ROPE_BASE ** (-i / PAIRS)
+        head = leading_bits(inv_freq, 24)
+        nc.vector.memset(freq_head[:, i : i + 1], head)
+        nc.vector.memset(freq_tail[:, i : i + 1], inv_freq - head)
+
+    coords_f = consts.tile([P, columns], F32)
+    nc.vector.tensor_copy(out=coords_f[:], in_=coords_bf[:].rearrange("p b a -> p (b a)"))
+
+    coords_wide = coords_f[:].unsqueeze(2).to_broadcast(shape)
+    angle = consts.tile(shape, F32)
+    angle_tail = consts.tile(shape, F32)
+    nc.vector.tensor_tensor(
+        out=angle[:], in0=coords_wide, in1=freq_head[:].unsqueeze(1).to_broadcast(shape), op=ALU.mult
+    )
+    nc.vector.tensor_tensor(
+        out=angle_tail[:], in0=coords_wide, in1=freq_tail[:].unsqueeze(1).to_broadcast(shape), op=ALU.mult
+    )
+    nc.vector.tensor_tensor(out=angle[:], in0=angle[:], in1=angle_tail[:], op=ALU.add)
+
+    turns = consts.tile(shape, F32)
+    nc.vector.tensor_scalar(
+        out=turns[:], in0=angle[:], scalar1=1.0 / (2.0 * math.pi), scalar2=ROUND_MAGIC, op0=ALU.mult, op1=ALU.add
+    )
+    nc.vector.tensor_scalar(out=turns[:], in0=turns[:], scalar1=ROUND_MAGIC, scalar2=None, op0=ALU.subtract)
+
+    y = consts.tile(shape, F32)
+    part1 = leading_bits(2.0 * math.pi, 12)
+    part2 = leading_bits(2.0 * math.pi - part1, 12)
+    part3 = 2.0 * math.pi - part1 - part2
+    flat = "p c i -> p (c i)"
+    nc.vector.scalar_tensor_tensor(
+        out=y[:].rearrange(flat), in0=turns[:].rearrange(flat), scalar=-part1, in1=angle[:].rearrange(flat),
+        op0=ALU.mult, op1=ALU.add,
+    )
+    for part in (part2, part3):
+        nc.vector.scalar_tensor_tensor(
+            out=y[:].rearrange(flat), in0=turns[:].rearrange(flat), scalar=-part, in1=y[:].rearrange(flat),
+            op0=ALU.mult, op1=ALU.add,
+        )
+    pi_below = int(math.pi * 2.0**22) / 2.0**22
+    nc.vector.tensor_scalar(out=y[:], in0=y[:], scalar1=pi_below, scalar2=-pi_below, op0=ALU.min, op1=ALU.max)
+
+    z = consts.tile(shape, F32)
+    half_pi_head = leading_bits(math.pi / 2.0, 24)
+    nc.vector.scalar_tensor_tensor(
+        out=z[:].rearrange(flat), in0=y[:].rearrange(flat), scalar=-1.0, in1=y[:].rearrange(flat),
+        op0=ALU.mult, op1=ALU.max,
+    )
+    nc.vector.tensor_scalar(out=z[:], in0=z[:], scalar1=-1.0, scalar2=half_pi_head, op0=ALU.mult, op1=ALU.add)
+    nc.vector.tensor_scalar(out=z[:], in0=z[:], scalar1=math.pi / 2.0 - half_pi_head, scalar2=None, op0=ALU.add)
+    return y, z
+
+
+def tile_crossattnrope_pa_k_kernel(tc, x_in, coords, w, out):
+    nc = tc.nc
+    with ExitStack() as ctx:
+        consts = ctx.enter_context(tc.tile_pool(name="consts", bufs=1))
+        raw_pool = ctx.enter_context(tc.tile_pool(name="raw", bufs=RAW_BUFS))
+        grouped_pool = ctx.enter_context(tc.tile_pool(name="grouped", bufs=2))
+        w_mx_pool = ctx.enter_context(tc.tile_pool(name="w_mx", bufs=3))
+        rope_pool = ctx.enter_context(tc.tile_pool(name="rope", bufs=2))
+        bank_pool = ctx.enter_context(tc.psum_pool(name="banks", bufs=TRANSPOSE_BANKS))
+        sum_pool = ctx.enter_context(tc.psum_pool(name="sums", bufs=1))
+        ctx.enter_context(tc.manual_schedule())
+
+        x_rows = x_in.rearrange("b l k -> l b k")
+        runs = [("x", 0), (0, 0), ("x", 1), (0, 1)]
+        runs.extend((group, half) for group in range(1, GROUPS) for half in range(HALVES))
+
+        def load(run):
+            owner, half = run
+            raw = raw_pool.tile([P, ROW_TILES * K_RUN], BF16)
+            k_cols = slice(half * K_RUN, (half + 1) * K_RUN)
+            if owner == "x":
+                rows = x_rows[:, :, k_cols]
+            else:
+                rows = w[owner * ROWS : (owner + 1) * ROWS, k_cols].rearrange("(j p) k -> p j k", p=P)
+            nc.sync.dma_start(out=raw[:].rearrange("p (j k) -> p j k", j=ROW_TILES), in_=rows)
+            return raw
+
+        coords_bf = consts.tile([P, BATCHES, AXES], BF16)
+        nc.scalar.dma_start(out=coords_bf[:], in_=coords.rearrange("b l a -> l b a"))
+        raw_tiles = [load(run) for run in runs[: RAW_BUFS - 1]]
+
+        zero = consts.tile([P, 1], F32)
+        nc.vector.memset(zero[:], 0.0)
+        warm = consts.tile([P, 1], F32)
+        nc.scalar.activation(out=warm[:], in_=zero[:], func=ACT.Sin)
+
+        identity = consts.tile([P, P], F32)
+        make_identity(nc, identity[:])
+
+        y, z = build_rotation_tables(nc, consts, coords_bf)
+        sin_table = consts.tile([P, BATCHES, AXES, PAIRS], F32)
+        minus_sin_table = consts.tile([P, BATCHES, AXES, PAIRS], F32)
+        cos_table = consts.tile([P, BATCHES, AXES, 2, PAIRS], F32)
+
+        x_codes = consts.tile([P, (K // K_PASS) * ROWS], U32, align_bytes=64)
+        x_scales = consts.tile([P, (K // K_PASS) * ROWS], U8, align_bytes=64)
+        product = consts.tile([P, BATCHES, FEATURES], F32)
+
+        def transpose_and_quantise(raw, codes, scales):
+            raw_words = raw[:].bitcast(F32)
+            grouped = grouped_pool.tile([P, PASSES_RUN * 4 * ROWS], BF16, align_bytes=64)
+            grouped_words = grouped[:].bitcast(F32)
+
+            def quantise_pair(first):
+                nc.vector.quantize_mx(
+                    out=codes[:, first * ROWS : first * ROWS + PAIR_WORDS].bitcast(FP8X4),
+                    scales=scales[:, first * ROWS : first * ROWS + PAIR_WORDS],
+                    in_=grouped[:, first * 4 * ROWS : (first + 2) * 4 * ROWS],
+                )
+
+            for g in range(PASSES_RUN):
+                bank = bank_pool.tile([P, BANK], F32)
+                for j in range(ROW_TILES):
+                    for u in range(2):
+                        first_word = j * (K_RUN // 2) + g * (K_PASS // 2) + u * P
+                        piece = (j * 2 + u) * P
+                        nc.tensor.transpose(
+                            bank[:, piece : piece + P], raw_words[:, first_word : first_word + P], identity[:]
+                        )
+                src = bank[:].rearrange("p (j u r) -> p j r u", j=ROW_TILES, u=2)
+                dst = grouped_words[:, g * BANK : (g + 1) * BANK].rearrange(
+                    "p (j r u) -> p j r u", j=ROW_TILES, u=2
+                )
+                if g == VECTOR_PASS:
+                    nc.vector.tensor_copy(out=dst, in_=src)
+                else:
+                    nc.scalar.copy(out=dst, in_=src)
+                if g % 2 == 1 and g >= 3:
+                    quantise_pair(g - 3)
+            quantise_pair(PASSES_RUN - 2)
+
+        def multiply(half, codes, scales, sums):
+            for b in range(BATCHES):
+                for g in range(PASSES_RUN):
+                    x_first = ((half * PASSES_RUN + g) * BATCHES + b) * P
+                    nc.tensor.matmul_mx(
+                        out=sums[b][:],
+                        lhsT=x_codes[:, x_first : x_first + P].bitcast(FP8X4),
+                        lhsT_scale=x_scales[:, x_first : x_first + P],
+                        rhs=codes[:, g * ROWS : (g + 1) * ROWS].bitcast(FP8X4),
+                        rhs_scale=scales[:, g * ROWS : (g + 1) * ROWS],
+                        start=(half == 0 and g == 0),
+                        stop=(half == HALVES - 1 and g == PASSES_RUN - 1),
+                    )
+
+        def rotate_and_store(first_head, end_head):
+            n = end_head - first_head
+            heads = product[:].rearrange("p b (h f) -> p b h f", f=HEAD_DIM)[:, :, first_head:end_head, :]
+            halves = product[:].rearrange("p b (h a s i) -> p b h a s i", a=AXES, s=2, i=PAIRS)
+            halves = halves[:, :, first_head:end_head]
+            rotated = rope_pool.tile([P, BATCHES, 3, HEAD_DIM], F32)
+            crossed = rope_pool.tile([P, BATCHES, 3, HEAD_DIM], F32)
+            crossed_halves = crossed[:].rearrange("p b h (a s i) -> p b h a s i", a=AXES, s=2)[:, :, :n]
+            pair_shape = [P, BATCHES, n, AXES, PAIRS]
+            nc.vector.tensor_tensor(
+                out=rotated[:, :, :n, :],
+                in0=heads,
+                in1=cos_table[:].rearrange("p b a s i -> p b (a s i)").unsqueeze(2).to_broadcast(
+                    [P, BATCHES, n, HEAD_DIM]
+                ),
+                op=ALU.mult,
+            )
+            nc.vector.tensor_tensor(
+                out=crossed_halves[:, :, :, :, 0, :],
+                in0=halves[:, :, :, :, 1, :],
+                in1=minus_sin_table[:].unsqueeze(2).to_broadcast(pair_shape),
+                op=ALU.mult,
+            )
+            nc.vector.tensor_tensor(
+                out=crossed_halves[:, :, :, :, 1, :],
+                in0=halves[:, :, :, :, 0, :],
+                in1=sin_table[:].unsqueeze(2).to_broadcast(pair_shape),
+                op=ALU.mult,
+            )
+            nc.vector.tensor_tensor(
+                out=rotated[:, :, :n, :], in0=rotated[:, :, :n, :], in1=crossed[:, :, :n, :], op=ALU.add
+            )
+            for b in range(BATCHES):
+                nc.gpsimd.dma_start(
+                    out=out[b, first_head:end_head].rearrange("h l d -> l h d"), in_=rotated[:, b, :n, :]
+                )
+
+        waiting = None
+        sums = None
+        for r, run in enumerate(runs):
+            owner, half = run
+            if r + RAW_BUFS - 1 < len(runs):
+                raw_tiles.append(load(runs[r + RAW_BUFS - 1]))
+            if owner == "x":
+                first = half * PASSES_RUN * ROWS
+                codes = x_codes[:, first : first + PASSES_RUN * ROWS]
+                scales = x_scales[:, first : first + PASSES_RUN * ROWS]
+            else:
+                w_codes = w_mx_pool.tile([P, PASSES_RUN * ROWS], U32, align_bytes=64)
+                w_scales = w_mx_pool.tile([P, PASSES_RUN * ROWS], U8, align_bytes=64)
+                codes, scales = w_codes[:], w_scales[:]
+            transpose_and_quantise(raw_tiles[r], codes, scales)
+
+            if r == 0:
+                flat = "p b a i -> p (b a) i"
+                nc.scalar.activation(out=sin_table[:].rearrange(flat), in_=y[:], func=ACT.Sin)
+                nc.scalar.activation(out=minus_sin_table[:].rearrange(flat), in_=y[:], func=ACT.Sin, scale=-1.0)
+                for s in range(2):
+                    nc.scalar.activation(out=cos_table[:, :, :, s, :].rearrange(flat), in_=z[:], func=ACT.Sin)
+
+            last = r == len(runs) - 1
+            for todo in ([waiting] if not last else [waiting, (owner, half, codes, scales)]):
+                if todo is None:
+                    continue
+                group, group_half, group_codes, group_scales = todo
+                if group_half == 0:
+                    sums = [
+                        sum_pool.tile([P, ROWS], F32, name="sum%d" % b, tag="sum%d" % b) for b in range(BATCHES)
+                    ]
+                multiply(group_half, group_codes, group_scales, sums)
+                if group_half == HALVES - 1:
+                    for b in range(BATCHES):
+                        nc.scalar.copy(out=product[:, b, group * ROWS : (group + 1) * ROWS], in_=sums[b][:])
+                    rotate_and_store(group * ROWS // HEAD_DIM, (group + 1) * ROWS // HEAD_DIM)
+            waiting = None if owner == "x" else (owner, half, codes, scales)

@@ -28,9 +28,12 @@ GROUPS = FEATURES // ROWS
 BANK = 512
 PAIR_WORDS = 2 * ROWS
 
-RAW_BUFS = 6
+LOADS_RUN = 2
+PASSES_LOAD = PASSES_RUN // LOADS_RUN
+K_LOAD = PASSES_LOAD * K_PASS
+RUNS_AHEAD = 5
 TRANSPOSE_BANKS = 6
-VECTOR_PASS = 3
+VECTOR_EVERY = 3
 
 FLOPS = 2 * BATCHES * TOKENS * FEATURES * K
 
@@ -110,7 +113,7 @@ def tile_crossattnrope_pa_k_kernel(tc, x_in, coords, w, out):
     nc = tc.nc
     with ExitStack() as ctx:
         consts = ctx.enter_context(tc.tile_pool(name="consts", bufs=1))
-        raw_pool = ctx.enter_context(tc.tile_pool(name="raw", bufs=RAW_BUFS))
+        raw_pool = ctx.enter_context(tc.tile_pool(name="raw", bufs=(RUNS_AHEAD + 1) * LOADS_RUN))
         grouped_pool = ctx.enter_context(tc.tile_pool(name="grouped", bufs=2))
         w_mx_pool = ctx.enter_context(tc.tile_pool(name="w_mx", bufs=3))
         rope_pool = ctx.enter_context(tc.tile_pool(name="rope", bufs=2))
@@ -124,18 +127,22 @@ def tile_crossattnrope_pa_k_kernel(tc, x_in, coords, w, out):
 
         def load(run):
             owner, half = run
-            raw = raw_pool.tile([P, ROW_TILES * K_RUN], BF16)
-            k_cols = slice(half * K_RUN, (half + 1) * K_RUN)
-            if owner == "x":
-                rows = x_rows[:, :, k_cols]
-            else:
-                rows = w[owner * ROWS : (owner + 1) * ROWS, k_cols].rearrange("(j p) k -> p j k", p=P)
-            nc.sync.dma_start(out=raw[:].rearrange("p (j k) -> p j k", j=ROW_TILES), in_=rows)
-            return raw
+            pieces = []
+            for c in range(LOADS_RUN):
+                raw = raw_pool.tile([P, ROW_TILES * K_LOAD], BF16)
+                first_k = half * K_RUN + c * K_LOAD
+                k_cols = slice(first_k, first_k + K_LOAD)
+                if owner == "x":
+                    rows = x_rows[:, :, k_cols]
+                else:
+                    rows = w[owner * ROWS : (owner + 1) * ROWS, k_cols].rearrange("(j p) k -> p j k", p=P)
+                nc.sync.dma_start(out=raw[:].rearrange("p (j k) -> p j k", j=ROW_TILES), in_=rows)
+                pieces.append(raw)
+            return pieces
 
         coords_bf = consts.tile([P, BATCHES, AXES], BF16)
         nc.scalar.dma_start(out=coords_bf[:], in_=coords.rearrange("b l a -> l b a"))
-        raw_tiles = [load(run) for run in runs[: RAW_BUFS - 1]]
+        raw_tiles = [load(run) for run in runs[:RUNS_AHEAD]]
 
         zero = consts.tile([P, 1], F32)
         nc.vector.memset(zero[:], 0.0)
@@ -154,8 +161,7 @@ def tile_crossattnrope_pa_k_kernel(tc, x_in, coords, w, out):
         x_scales = consts.tile([P, (K // K_PASS) * ROWS], U8, align_bytes=64)
         product = consts.tile([P, BATCHES, FEATURES], F32)
 
-        def transpose_and_quantise(raw, codes, scales):
-            raw_words = raw[:].bitcast(F32)
+        def transpose_and_quantise(pieces, codes, scales):
             grouped = grouped_pool.tile([P, PASSES_RUN * 4 * ROWS], BF16, align_bytes=64)
             grouped_words = grouped[:].bitcast(F32)
 
@@ -168,9 +174,10 @@ def tile_crossattnrope_pa_k_kernel(tc, x_in, coords, w, out):
 
             for g in range(PASSES_RUN):
                 bank = bank_pool.tile([P, BANK], F32)
+                raw_words = pieces[g // PASSES_LOAD][:].bitcast(F32)
                 for j in range(ROW_TILES):
                     for u in range(2):
-                        first_word = j * (K_RUN // 2) + g * (K_PASS // 2) + u * P
+                        first_word = j * (K_LOAD // 2) + (g % PASSES_LOAD) * (K_PASS // 2) + u * P
                         piece = (j * 2 + u) * P
                         nc.tensor.transpose(
                             bank[:, piece : piece + P], raw_words[:, first_word : first_word + P], identity[:]
@@ -179,7 +186,7 @@ def tile_crossattnrope_pa_k_kernel(tc, x_in, coords, w, out):
                 dst = grouped_words[:, g * BANK : (g + 1) * BANK].rearrange(
                     "p (j r u) -> p j r u", j=ROW_TILES, u=2
                 )
-                if g == VECTOR_PASS:
+                if g % VECTOR_EVERY == VECTOR_EVERY - 1:
                     nc.vector.tensor_copy(out=dst, in_=src)
                 else:
                     nc.scalar.copy(out=dst, in_=src)
@@ -201,40 +208,42 @@ def tile_crossattnrope_pa_k_kernel(tc, x_in, coords, w, out):
                         stop=(half == HALVES - 1 and g == PASSES_RUN - 1),
                     )
 
-        def rotate_and_store(first_head, end_head):
+        def rotate_and_store(first_head, end_head, first_batch, end_batch, queue):
             n = end_head - first_head
-            heads = product[:].rearrange("p b (h f) -> p b h f", f=HEAD_DIM)[:, :, first_head:end_head, :]
+            bs = slice(first_batch, end_batch)
+            nb = end_batch - first_batch
+            heads = product[:].rearrange("p b (h f) -> p b h f", f=HEAD_DIM)[:, bs, first_head:end_head, :]
             halves = product[:].rearrange("p b (h a s i) -> p b h a s i", a=AXES, s=2, i=PAIRS)
-            halves = halves[:, :, first_head:end_head]
+            halves = halves[:, bs, first_head:end_head]
             rotated = rope_pool.tile([P, BATCHES, 3, HEAD_DIM], F32)
             crossed = rope_pool.tile([P, BATCHES, 3, HEAD_DIM], F32)
-            crossed_halves = crossed[:].rearrange("p b h (a s i) -> p b h a s i", a=AXES, s=2)[:, :, :n]
-            pair_shape = [P, BATCHES, n, AXES, PAIRS]
+            crossed_halves = crossed[:].rearrange("p b h (a s i) -> p b h a s i", a=AXES, s=2)[:, bs, :n]
+            pair_shape = [P, nb, n, AXES, PAIRS]
             nc.vector.tensor_tensor(
-                out=rotated[:, :, :n, :],
+                out=rotated[:, bs, :n, :],
                 in0=heads,
-                in1=cos_table[:].rearrange("p b a s i -> p b (a s i)").unsqueeze(2).to_broadcast(
-                    [P, BATCHES, n, HEAD_DIM]
+                in1=cos_table[:, bs].rearrange("p b a s i -> p b (a s i)").unsqueeze(2).to_broadcast(
+                    [P, nb, n, HEAD_DIM]
                 ),
                 op=ALU.mult,
             )
             nc.vector.tensor_tensor(
                 out=crossed_halves[:, :, :, :, 0, :],
                 in0=halves[:, :, :, :, 1, :],
-                in1=minus_sin_table[:].unsqueeze(2).to_broadcast(pair_shape),
+                in1=minus_sin_table[:, bs].unsqueeze(2).to_broadcast(pair_shape),
                 op=ALU.mult,
             )
             nc.vector.tensor_tensor(
                 out=crossed_halves[:, :, :, :, 1, :],
                 in0=halves[:, :, :, :, 0, :],
-                in1=sin_table[:].unsqueeze(2).to_broadcast(pair_shape),
+                in1=sin_table[:, bs].unsqueeze(2).to_broadcast(pair_shape),
                 op=ALU.mult,
             )
             nc.vector.tensor_tensor(
-                out=rotated[:, :, :n, :], in0=rotated[:, :, :n, :], in1=crossed[:, :, :n, :], op=ALU.add
+                out=rotated[:, bs, :n, :], in0=rotated[:, bs, :n, :], in1=crossed[:, bs, :n, :], op=ALU.add
             )
-            for b in range(BATCHES):
-                nc.gpsimd.dma_start(
+            for b in range(first_batch, end_batch):
+                queue.dma_start(
                     out=out[b, first_head:end_head].rearrange("h l d -> l h d"), in_=rotated[:, b, :n, :]
                 )
 
@@ -242,8 +251,8 @@ def tile_crossattnrope_pa_k_kernel(tc, x_in, coords, w, out):
         sums = None
         for r, run in enumerate(runs):
             owner, half = run
-            if r + RAW_BUFS - 1 < len(runs):
-                raw_tiles.append(load(runs[r + RAW_BUFS - 1]))
+            if r + RUNS_AHEAD < len(runs):
+                raw_tiles.append(load(runs[r + RUNS_AHEAD]))
             if owner == "x":
                 first = half * PASSES_RUN * ROWS
                 codes = x_codes[:, first : first + PASSES_RUN * ROWS]
@@ -274,5 +283,10 @@ def tile_crossattnrope_pa_k_kernel(tc, x_in, coords, w, out):
                 if group_half == HALVES - 1:
                     for b in range(BATCHES):
                         nc.scalar.copy(out=product[:, b, group * ROWS : (group + 1) * ROWS], in_=sums[b][:])
-                    rotate_and_store(group * ROWS // HEAD_DIM, (group + 1) * ROWS // HEAD_DIM)
+                    first_head, end_head = group * ROWS // HEAD_DIM, (group + 1) * ROWS // HEAD_DIM
+                    if group < GROUPS - 1:
+                        rotate_and_store(first_head, end_head, 0, BATCHES, nc.gpsimd)
+                    else:
+                        for b in range(BATCHES):
+                            rotate_and_store(first_head, end_head, b, b + 1, nc.sync)
             waiting = None if owner == "x" else (owner, half, codes, scales)

@@ -21,17 +21,17 @@ ROPE_BASE = 10000.0
 K_PASS = 512
 ROWS = 256
 ROW_TILES = ROWS // P
-PASSES_RUN = 8
+PASSES_RUN = 4
 K_RUN = PASSES_RUN * K_PASS
-HALVES = K // K_RUN
+PARTS = K // K_RUN
 GROUPS = FEATURES // ROWS
 BANK = 512
 PAIR_WORDS = 2 * ROWS
 
-LOADS_RUN = 2
+LOADS_RUN = 1
 PASSES_LOAD = PASSES_RUN // LOADS_RUN
 K_LOAD = PASSES_LOAD * K_PASS
-RUNS_AHEAD = 5
+RUNS_AHEAD = 11
 TRANSPOSE_BANKS = 6
 VECTOR_EVERY = 3
 
@@ -114,23 +114,25 @@ def tile_crossattnrope_pa_k_kernel(tc, x_in, coords, w, out):
     with ExitStack() as ctx:
         consts = ctx.enter_context(tc.tile_pool(name="consts", bufs=1))
         raw_pool = ctx.enter_context(tc.tile_pool(name="raw", bufs=(RUNS_AHEAD + 1) * LOADS_RUN))
-        grouped_pool = ctx.enter_context(tc.tile_pool(name="grouped", bufs=2))
-        w_mx_pool = ctx.enter_context(tc.tile_pool(name="w_mx", bufs=3))
+        grouped_pool = ctx.enter_context(tc.tile_pool(name="grouped", bufs=4))
+        w_mx_pool = ctx.enter_context(tc.tile_pool(name="w_mx", bufs=4))
         rope_pool = ctx.enter_context(tc.tile_pool(name="rope", bufs=2))
         bank_pool = ctx.enter_context(tc.psum_pool(name="banks", bufs=TRANSPOSE_BANKS))
         sum_pool = ctx.enter_context(tc.psum_pool(name="sums", bufs=1))
         ctx.enter_context(tc.manual_schedule())
 
         x_rows = x_in.rearrange("b l k -> l b k")
-        runs = [("x", 0), (0, 0), ("x", 1), (0, 1)]
-        runs.extend((group, half) for group in range(1, GROUPS) for half in range(HALVES))
+        runs = []
+        for part in range(PARTS):
+            runs.extend([("x", part), (0, part)])
+        runs.extend((group, part) for group in range(1, GROUPS) for part in range(PARTS))
 
         def load(run):
-            owner, half = run
+            owner, part = run
             pieces = []
             for c in range(LOADS_RUN):
                 raw = raw_pool.tile([P, ROW_TILES * K_LOAD], BF16)
-                first_k = half * K_RUN + c * K_LOAD
+                first_k = part * K_RUN + c * K_LOAD
                 k_cols = slice(first_k, first_k + K_LOAD)
                 if owner == "x":
                     rows = x_rows[:, :, k_cols]
@@ -194,18 +196,18 @@ def tile_crossattnrope_pa_k_kernel(tc, x_in, coords, w, out):
                     quantise_pair(g - 3)
             quantise_pair(PASSES_RUN - 2)
 
-        def multiply(half, codes, scales, sums):
+        def multiply(part, codes, scales, sums):
             for b in range(BATCHES):
                 for g in range(PASSES_RUN):
-                    x_first = ((half * PASSES_RUN + g) * BATCHES + b) * P
+                    x_first = ((part * PASSES_RUN + g) * BATCHES + b) * P
                     nc.tensor.matmul_mx(
                         out=sums[b][:],
                         lhsT=x_codes[:, x_first : x_first + P].bitcast(FP8X4),
                         lhsT_scale=x_scales[:, x_first : x_first + P],
                         rhs=codes[:, g * ROWS : (g + 1) * ROWS].bitcast(FP8X4),
                         rhs_scale=scales[:, g * ROWS : (g + 1) * ROWS],
-                        start=(half == 0 and g == 0),
-                        stop=(half == HALVES - 1 and g == PASSES_RUN - 1),
+                        start=(part == 0 and g == 0),
+                        stop=(part == PARTS - 1 and g == PASSES_RUN - 1),
                     )
 
         def rotate_and_store(first_head, end_head, first_batch, end_batch, queue):
@@ -250,11 +252,11 @@ def tile_crossattnrope_pa_k_kernel(tc, x_in, coords, w, out):
         waiting = None
         sums = None
         for r, run in enumerate(runs):
-            owner, half = run
+            owner, part = run
             if r + RUNS_AHEAD < len(runs):
                 raw_tiles.append(load(runs[r + RUNS_AHEAD]))
             if owner == "x":
-                first = half * PASSES_RUN * ROWS
+                first = part * PASSES_RUN * ROWS
                 codes = x_codes[:, first : first + PASSES_RUN * ROWS]
                 scales = x_scales[:, first : first + PASSES_RUN * ROWS]
             else:
@@ -271,16 +273,16 @@ def tile_crossattnrope_pa_k_kernel(tc, x_in, coords, w, out):
                     nc.scalar.activation(out=cos_table[:, :, :, s, :].rearrange(flat), in_=z[:], func=ACT.Sin)
 
             last = r == len(runs) - 1
-            for todo in ([waiting] if not last else [waiting, (owner, half, codes, scales)]):
+            for todo in ([waiting] if not last else [waiting, (owner, part, codes, scales)]):
                 if todo is None:
                     continue
-                group, group_half, group_codes, group_scales = todo
-                if group_half == 0:
+                group, group_part, group_codes, group_scales = todo
+                if group_part == 0:
                     sums = [
                         sum_pool.tile([P, ROWS], F32, name="sum%d" % b, tag="sum%d" % b) for b in range(BATCHES)
                     ]
-                multiply(group_half, group_codes, group_scales, sums)
-                if group_half == HALVES - 1:
+                multiply(group_part, group_codes, group_scales, sums)
+                if group_part == PARTS - 1:
                     for b in range(BATCHES):
                         nc.scalar.copy(out=product[:, b, group * ROWS : (group + 1) * ROWS], in_=sums[b][:])
                     first_head, end_head = group * ROWS // HEAD_DIM, (group + 1) * ROWS // HEAD_DIM
@@ -289,4 +291,4 @@ def tile_crossattnrope_pa_k_kernel(tc, x_in, coords, w, out):
                     else:
                         for b in range(BATCHES):
                             rotate_and_store(first_head, end_head, b, b + 1, nc.sync)
-            waiting = None if owner == "x" else (owner, half, codes, scales)
+            waiting = None if owner == "x" else (owner, part, codes, scales)

from contextlib import ExitStack
import math

import concourse.mybir as mybir
from concourse.masks import make_identity

F32 = mybir.dt.float32
BF16 = mybir.dt.bfloat16
U32 = mybir.dt.uint32
U8 = mybir.dt.uint8
FP8X4 = mybir.dt.float8_e4m3fn_x4
ALU = mybir.AluOpType
ACT = mybir.ActivationFunctionType

P = 128
BATCHES, TOKENS, K = 2, 128, 8192
HEADS, HEAD_DIM, AXES, PAIRS = 16, 96, 3, 16
FEATURES = HEADS * HEAD_DIM
ROPE_BASE = 10000.0

K_PASS = 512
ROWS = 256
ROW_TILES = ROWS // P
PASSES_RUN = 4
K_RUN = PASSES_RUN * K_PASS
PARTS = K // K_RUN
GROUPS = FEATURES // ROWS
BANK = 512
PAIR_WORDS = 2 * ROWS

LOADS_RUN = 1
PASSES_LOAD = PASSES_RUN // LOADS_RUN
K_LOAD = PASSES_LOAD * K_PASS
RUNS_AHEAD = 11
TRANSPOSE_BANKS = 6
VECTOR_EVERY = 3

FLOPS = 2 * BATCHES * TOKENS * FEATURES * K

ROUND_MAGIC = 1.5 * 2.0**23


def leading_bits(value, bits):
    scale = 1.0
    while abs(value) * scale < 2.0 ** (bits - 1):
        scale *= 2.0
    while abs(value) * scale >= 2.0**bits:
        scale /= 2.0
    return round(value * scale) / scale


def build_rotation_tables(nc, consts, coords_bf):
    columns = BATCHES * AXES
    shape = [P, columns, PAIRS]

    freq_head = consts.tile([P, PAIRS], F32)
    freq_tail = consts.tile([P, PAIRS], F32)
    for i in range(PAIRS):
        inv_freq = ROPE_BASE ** (-i / PAIRS)
        head = leading_bits(inv_freq, 24)
        nc.vector.memset(freq_head[:, i : i + 1], head)
        nc.vector.memset(freq_tail[:, i : i + 1], inv_freq - head)

    coords_f = consts.tile([P, columns], F32)
    nc.vector.tensor_copy(out=coords_f[:], in_=coords_bf[:].rearrange("p b a -> p (b a)"))

    coords_wide = coords_f[:].unsqueeze(2).to_broadcast(shape)
    angle = consts.tile(shape, F32)
    angle_tail = consts.tile(shape, F32)
    nc.vector.tensor_tensor(
        out=angle[:], in0=coords_wide, in1=freq_head[:].unsqueeze(1).to_broadcast(shape), op=ALU.mult
    )
    nc.vector.tensor_tensor(
        out=angle_tail[:], in0=coords_wide, in1=freq_tail[:].unsqueeze(1).to_broadcast(shape), op=ALU.mult
    )
    nc.vector.tensor_tensor(out=angle[:], in0=angle[:], in1=angle_tail[:], op=ALU.add)

    turns = consts.tile(shape, F32)
    nc.vector.tensor_scalar(
        out=turns[:], in0=angle[:], scalar1=1.0 / (2.0 * math.pi), scalar2=ROUND_MAGIC, op0=ALU.mult, op1=ALU.add
    )
    nc.vector.tensor_scalar(out=turns[:], in0=turns[:], scalar1=ROUND_MAGIC, scalar2=None, op0=ALU.subtract)

    y = consts.tile(shape, F32)
    part1 = leading_bits(2.0 * math.pi, 12)
    part2 = leading_bits(2.0 * math.pi - part1, 12)
    part3 = 2.0 * math.pi - part1 - part2
    flat = "p c i -> p (c i)"
    nc.vector.scalar_tensor_tensor(
        out=y[:].rearrange(flat), in0=turns[:].rearrange(flat), scalar=-part1, in1=angle[:].rearrange(flat),
        op0=ALU.mult, op1=ALU.add,
    )
    for part in (part2, part3):
        nc.vector.scalar_tensor_tensor(
            out=y[:].rearrange(flat), in0=turns[:].rearrange(flat), scalar=-part, in1=y[:].rearrange(flat),
            op0=ALU.mult, op1=ALU.add,
        )
    pi_below = int(math.pi * 2.0**22) / 2.0**22
    nc.vector.tensor_scalar(out=y[:], in0=y[:], scalar1=pi_below, scalar2=-pi_below, op0=ALU.min, op1=ALU.max)

    z = consts.tile(shape, F32)
    half_pi_head = leading_bits(math.pi / 2.0, 24)
    nc.vector.scalar_tensor_tensor(
        out=z[:].rearrange(flat), in0=y[:].rearrange(flat), scalar=-1.0, in1=y[:].rearrange(flat),
        op0=ALU.mult, op1=ALU.max,
    )
    nc.vector.tensor_scalar(out=z[:], in0=z[:], scalar1=-1.0, scalar2=half_pi_head, op0=ALU.mult, op1=ALU.add)
    nc.vector.tensor_scalar(out=z[:], in0=z[:], scalar1=math.pi / 2.0 - half_pi_head, scalar2=None, op0=ALU.add)
    return y, z


def tile_crossattnrope_pa_k_kernel(tc, x_in, coords, w, out):
    nc = tc.nc
    with ExitStack() as ctx:
        consts = ctx.enter_context(tc.tile_pool(name="consts", bufs=1))
        raw_pool = ctx.enter_context(tc.tile_pool(name="raw", bufs=(RUNS_AHEAD + 1) * LOADS_RUN))
        grouped_pool = ctx.enter_context(tc.tile_pool(name="grouped", bufs=4))
        w_mx_pool = ctx.enter_context(tc.tile_pool(name="w_mx", bufs=4))
        rope_pool = ctx.enter_context(tc.tile_pool(name="rope", bufs=2))
        bank_pool = ctx.enter_context(tc.psum_pool(name="banks", bufs=TRANSPOSE_BANKS))
        sum_pool = ctx.enter_context(tc.psum_pool(name="sums", bufs=1))
        ctx.enter_context(tc.manual_schedule())

        x_rows = x_in.rearrange("b l k -> l b k")
        runs = []
        for part in range(PARTS):
            runs.extend([("x", part), (0, part)])
        runs.extend((group, part) for group in range(1, GROUPS) for part in range(PARTS))

        def load(run):
            owner, part = run
            pieces = []
            for c in range(LOADS_RUN):
                raw = raw_pool.tile([P, ROW_TILES * K_LOAD], BF16)
                first_k = part * K_RUN + c * K_LOAD
                k_cols = slice(first_k, first_k + K_LOAD)
                if owner == "x":
                    rows = x_rows[:, :, k_cols]
                else:
                    rows = w[owner * ROWS : (owner + 1) * ROWS, k_cols].rearrange("(j p) k -> p j k", p=P)
                nc.sync.dma_start(out=raw[:].rearrange("p (j k) -> p j k", j=ROW_TILES), in_=rows)
                pieces.append(raw)
            return pieces

        coords_bf = consts.tile([P, BATCHES, AXES], BF16)
        nc.scalar.dma_start(out=coords_bf[:], in_=coords.rearrange("b l a -> l b a"))
        raw_tiles = [load(run) for run in runs[:RUNS_AHEAD]]

        zero = consts.tile([P, 1], F32)
        nc.vector.memset(zero[:], 0.0)
        warm = consts.tile([P, 1], F32)
        nc.scalar.activation(out=warm[:], in_=zero[:], func=ACT.Sin)

        identity = consts.tile([P, P], F32)
        make_identity(nc, identity[:])

        y, z = build_rotation_tables(nc, consts, coords_bf)
        sin_table = consts.tile([P, BATCHES, AXES, PAIRS], F32)
        minus_sin_table = consts.tile([P, BATCHES, AXES, PAIRS], F32)
        cos_table = consts.tile([P, BATCHES, AXES, 2, PAIRS], F32)

        x_codes = consts.tile([P, (K // K_PASS) * ROWS], U32, align_bytes=64)
        x_scales = consts.tile([P, (K // K_PASS) * ROWS], U8, align_bytes=64)
        product = consts.tile([P, BATCHES, FEATURES], F32)

        def transpose_and_quantise(pieces, codes, scales):
            grouped = grouped_pool.tile([P, PASSES_RUN * 4 * ROWS], BF16, align_bytes=64)
            grouped_words = grouped[:].bitcast(F32)

            def quantise_pair(first):
                nc.vector.quantize_mx(
                    out=codes[:, first * ROWS : first * ROWS + PAIR_WORDS].bitcast(FP8X4),
                    scales=scales[:, first * ROWS : first * ROWS + PAIR_WORDS],
                    in_=grouped[:, first * 4 * ROWS : (first + 2) * 4 * ROWS],
                )

            for g in range(PASSES_RUN):
                bank = bank_pool.tile([P, BANK], F32)
                raw_words = pieces[g // PASSES_LOAD][:].bitcast(F32)
                for j in range(ROW_TILES):
                    for u in range(2):
                        first_word = j * (K_LOAD // 2) + (g % PASSES_LOAD) * (K_PASS // 2) + u * P
                        piece = (j * 2 + u) * P
                        nc.tensor.transpose(
                            bank[:, piece : piece + P], raw_words[:, first_word : first_word + P], identity[:]
                        )
                src = bank[:].rearrange("p (j u r) -> p j r u", j=ROW_TILES, u=2)
                dst = grouped_words[:, g * BANK : (g + 1) * BANK].rearrange(
                    "p (j r u) -> p j r u", j=ROW_TILES, u=2
                )
                if g % VECTOR_EVERY == VECTOR_EVERY - 1:
                    nc.vector.tensor_copy(out=dst, in_=src)
                else:
                    nc.scalar.copy(out=dst, in_=src)
                if g % 2 == 1 and g >= 3:
                    quantise_pair(g - 3)
            quantise_pair(PASSES_RUN - 2)

        def multiply(part, codes, scales, sums):
            for b in range(BATCHES):
                for g in range(PASSES_RUN):
                    x_first = ((part * PASSES_RUN + g) * BATCHES + b) * P
                    nc.tensor.matmul_mx(
                        out=sums[b][:],
                        lhsT=x_codes[:, x_first : x_first + P].bitcast(FP8X4),
                        lhsT_scale=x_scales[:, x_first : x_first + P],
                        rhs=codes[:, g * ROWS : (g + 1) * ROWS].bitcast(FP8X4),
                        rhs_scale=scales[:, g * ROWS : (g + 1) * ROWS],
                        start=(part == 0 and g == 0),
                        stop=(part == PARTS - 1 and g == PASSES_RUN - 1),
                    )

        def rotate_and_store(first_head, end_head, first_batch, end_batch, queue):
            n = end_head - first_head
            bs = slice(first_batch, end_batch)
            nb = end_batch - first_batch
            heads = product[:].rearrange("p b (h f) -> p b h f", f=HEAD_DIM)[:, bs, first_head:end_head, :]
            halves = product[:].rearrange("p b (h a s i) -> p b h a s i", a=AXES, s=2, i=PAIRS)
            halves = halves[:, bs, first_head:end_head]
            rotated = rope_pool.tile([P, BATCHES, 3, HEAD_DIM], F32)
            crossed = rope_pool.tile([P, BATCHES, 3, HEAD_DIM], F32)
            crossed_halves = crossed[:].rearrange("p b h (a s i) -> p b h a s i", a=AXES, s=2)[:, bs, :n]
            pair_shape = [P, nb, n, AXES, PAIRS]
            nc.vector.tensor_tensor(
                out=rotated[:, bs, :n, :],
                in0=heads,
                in1=cos_table[:, bs].rearrange("p b a s i -> p b (a s i)").unsqueeze(2).to_broadcast(
                    [P, nb, n, HEAD_DIM]
                ),
                op=ALU.mult,
            )
            nc.vector.tensor_tensor(
                out=crossed_halves[:, :, :, :, 0, :],
                in0=halves[:, :, :, :, 1, :],
                in1=minus_sin_table[:, bs].unsqueeze(2).to_broadcast(pair_shape),
                op=ALU.mult,
            )
            nc.vector.tensor_tensor(
                out=crossed_halves[:, :, :, :, 1, :],
                in0=halves[:, :, :, :, 0, :],
                in1=sin_table[:, bs].unsqueeze(2).to_broadcast(pair_shape),
                op=ALU.mult,
            )
            nc.vector.tensor_tensor(
                out=rotated[:, bs, :n, :], in0=rotated[:, bs, :n, :], in1=crossed[:, bs, :n, :], op=ALU.add
            )
            for b in range(first_batch, end_batch):
                queue.dma_start(
                    out=out[b, first_head:end_head].rearrange("h l d -> l h d"), in_=rotated[:, b, :n, :]
                )

        waiting = None
        sums = None
        for r, run in enumerate(runs):
            owner, part = run
            if r + RUNS_AHEAD < len(runs):
                raw_tiles.append(load(runs[r + RUNS_AHEAD]))
            if owner == "x":
                first = part * PASSES_RUN * ROWS
                codes = x_codes[:, first : first + PASSES_RUN * ROWS]
                scales = x_scales[:, first : first + PASSES_RUN * ROWS]
            else:
                w_codes = w_mx_pool.tile([P, PASSES_RUN * ROWS], U32, align_bytes=64)
                w_scales = w_mx_pool.tile([P, PASSES_RUN * ROWS], U8, align_bytes=64)
                codes, scales = w_codes[:], w_scales[:]
            transpose_and_quantise(raw_tiles[r], codes, scales)

            if r == 0:
                flat = "p b a i -> p (b a) i"
                nc.scalar.activation(out=sin_table[:].rearrange(flat), in_=y[:], func=ACT.Sin)
                nc.scalar.activation(out=minus_sin_table[:].rearrange(flat), in_=y[:], func=ACT.Sin, scale=-1.0)
                for s in range(2):
                    nc.scalar.activation(out=cos_table[:, :, :, s, :].rearrange(flat), in_=z[:], func=ACT.Sin)

            last = r == len(runs) - 1
            for todo in ([waiting] if not last else [waiting, (owner, part, codes, scales)]):
                if todo is None:
                    continue
                group, group_part, group_codes, group_scales = todo
                if group_part == 0:
                    sums = [
                        sum_pool.tile([P, ROWS], F32, name="sum%d" % b, tag="sum%d" % b) for b in range(BATCHES)
                    ]
                multiply(group_part, group_codes, group_scales, sums)
                if group_part == PARTS - 1:
                    for b in range(BATCHES):
                        nc.scalar.copy(out=product[:, b, group * ROWS : (group + 1) * ROWS], in_=sums[b][:])
                    first_head, end_head = group * ROWS // HEAD_DIM, (group + 1) * ROWS // HEAD_DIM
                    if group < GROUPS - 1:
                        rotate_and_store(first_head, end_head, 0, BATCHES, nc.gpsimd)
                    else:
                        for b in range(BATCHES):
                            rotate_and_store(first_head, end_head, b, b + 1, nc.sync)
            waiting = None if owner == "x" else (owner, part, codes, scales)
